import numpy as np
import ml_dtypes


def mxq(x, axis, fmt="e4m3"):
    dtype, down = {"e4m3": (ml_dtypes.float8_e4m3fn, 7), "e5m2": (ml_dtypes.float8_e5m2, 14)}[fmt]
    v = np.moveaxis(np.asarray(x, np.float32).astype(ml_dtypes.bfloat16).astype(np.float64), axis, -1)
    blocks = v.reshape(v.shape[:-1] + (-1, 32))
    amax = np.abs(blocks).max(-1, keepdims=True)
    byte = np.maximum(np.where(amax > 0, np.frexp(amax)[1] - 1 + 127, 0) - down, 1)
    scale = np.exp2(byte - 127.0)
    codes = (blocks / scale).astype(np.float32).astype(dtype).astype(np.float64)
    return np.moveaxis((codes * scale).reshape(v.shape), -1, axis)


WIDE = False


def mx_kscale(k):
    if not WIDE:
        return np.ones(k)
    levels = np.array([10, -10, 5, -5, 0])
    a = np.random.permutation(np.resize(levels, k // 512 * 4)).reshape(k // 512, 4)
    idx = np.arange(k)
    return np.exp2(a[idx // 512, idx % 128 // 32])


BF16 = ml_dtypes.bfloat16


def bf(x):
    return np.asarray(x, np.float32).astype(BF16)


def f64(x):
    return np.asarray(x).astype(np.float64)


B, N, D, DO, H, HID = 12, 128, 512, 512, 8, 2048


def setup_inputs():
    s, t = mx_kscale(D), mx_kscale(D)
    adj = np.random.uniform(size=(N, N))
    adj = adj / adj.sum(-1, keepdims=True)
    return {
        "h_norm": bf(np.random.standard_normal((B, N, D)) * s),
        "o_attn": bf(np.random.standard_normal((B, N, D)) * 0.25 * t),
        "a_gcn": bf(adj + np.random.standard_normal((N, N)) * 0.5 / np.sqrt(N)),
        "w_proj": bf(np.random.standard_normal((D, DO)) * 2.0 / np.sqrt(D) / t[:, None]),
        "b_proj": bf(np.random.standard_normal(DO) * 0.1),
        "gcn_w": bf(np.random.standard_normal((D, DO)) / np.sqrt(D) / s[:, None]),
        "gcn_m": bf(1.0 + 0.1 * np.random.standard_normal(DO)),
    }


def reference(h_norm, o_attn, a_gcn, w_proj, b_proj, gcn_w, gcn_m):
    o = (mxq(f64(o_attn), 2, "e4m3") @ mxq(f64(w_proj), 0, "e4m3")) + f64(b_proj)
    agg = f64(a_gcn) @ f64(h_norm)
    g = (mxq(agg, 2, "e4m3") @ mxq(f64(gcn_w), 0, "e4m3")) * f64(gcn_m)
    return o + g

@@ -1,0 +1,214 @@
+from contextlib import ExitStack
+
+import concourse.mybir as mybir
+from concourse.masks import make_identity
+
+FP8X4 = mybir.dt.float8_e4m3fn_x4
+BF16 = mybir.dt.bfloat16
+F32 = mybir.dt.float32
+U32 = mybir.dt.uint32
+U8 = mybir.dt.uint8
+ADD = mybir.AluOpType.add
+MULT = mybir.AluOpType.mult
+
+P = 128
+B = 12
+D = 512
+PAIRS = B // 2
+FLOPS = 2 * B * P * D * D * 2 + 2 * B * P * P * D
+
+WP_S_COLS = 160
+GW_S_COLS = 128
+VECTOR_ADDS = (11,)
+
+
+def tile_gatblock_pa_kernel(tc, h_norm, o_attn, a_gcn, w_proj, b_proj, gcn_w, gcn_m, out):
+    nc = tc.nc
+    with ExitStack() as ctx:
+        keep = ctx.enter_context(tc.tile_pool(name="keep", bufs=1))
+        psum = ctx.enter_context(tc.psum_pool(name="psum", bufs=1))
+        ctx.enter_context(tc.manual_schedule())
+
+        rows = keep.tile([P, 2 * D], BF16, name="rows")
+        ones = keep.tile([P, P], BF16, name="ones")
+        ident_bf = keep.tile([P, P], BF16, name="ident_bf")
+        ident_f = keep.tile([P, P], F32, name="ident_f")
+        nc.vector.memset(rows[:], 0.0)
+        nc.vector.memset(ones[:], 1.0)
+        make_identity(nc, ident_f[:])
+        make_identity(nc, ident_bf[:])
+
+        wp_raw = keep.tile([P, 4, D], BF16, name="wp_raw")
+        gw_raw = keep.tile([P, 4, D], BF16, name="gw_raw")
+        a_sb = keep.tile([P, P], BF16, name="a_sb")
+        o_sb = [keep.tile([P, 2 * D], BF16, name="o_sb%d" % j) for j in range(PAIRS)]
+        h_sb = [keep.tile([P, 2, D], BF16, name="h_sb%d" % j) for j in range(PAIRS)]
+
+        def load_o(j):
+            nc.sync.dma_start(
+                out=o_sb[j][:].rearrange("p (s d) -> p s d", s=2),
+                in_=o_attn[2 * j : 2 * j + 2].rearrange("s n d -> n s d"),
+            )
+
+        def load_h(j):
+            nc.sync.dma_start(out=h_sb[j][:], in_=h_norm[2 * j : 2 * j + 2].rearrange("s n d -> n s d"))
+
+        nc.sync.dma_start(
+            out=wp_raw[:].rearrange("p (u e) c -> p u e c", u=2),
+            in_=w_proj.rearrange("(u p e) c -> p u e c", u=2, p=P, e=2),
+        )
+        nc.scalar.dma_start(out=a_sb[:], in_=a_gcn)
+        nc.scalar.dma_start(out=rows[0:1, 0:D], in_=b_proj.rearrange("(o n) -> o n", o=1))
+        nc.scalar.dma_start(out=rows[0:1, D : 2 * D], in_=gcn_m.rearrange("(o n) -> o n", o=1))
+        load_o(0)
+        nc.sync.dma_start(out=gw_raw[:], in_=gcn_w.rearrange("(t p) c -> p t c", t=4, p=P))
+        load_h(0)
+        for j in range(1, PAIRS):
+            load_o(j)
+            load_h(j)
+
+        def regroup(engine_copy, grp, raw, c0, c1):
+            engine_copy(
+                out=grp[:, c0:c1, :].rearrange("p (c i) t -> p c t i", i=4),
+                in_=raw[:, :, c0:c1].rearrange("p t (c i) -> p c t i", i=4),
+            )
+
+        wp_grp = keep.tile([P, D, 4], BF16, name="wp_grp", align_bytes=64)
+        gw_grp = keep.tile([P, D, 4], BF16, name="gw_grp", align_bytes=64)
+        wp_codes = keep.tile([P, D], U32, name="wp_codes", align_bytes=64)
+        gw_codes = keep.tile([P, D], U32, name="gw_codes", align_bytes=64)
+        wp_scales = keep.tile([P, D], U8, name="wp_scales", align_bytes=64)
+        gw_scales = keep.tile([P, D], U8, name="gw_scales", align_bytes=64)
+
+        def quantise(codes, scales, grouped):
+            nc.vector.quantize_mx(out=codes.bitcast(FP8X4), scales=scales, in_=grouped)
+
+        go = [keep.tile([P, 2 * D], BF16, name="go%d" % j, align_bytes=64) for j in range(PAIRS)]
+        ga = [keep.tile([P, 2 * D], BF16, name="ga%d" % j, align_bytes=64) for j in range(PAIRS)]
+        co = [keep.tile([P, 2 * P], U32, name="co%d" % j, align_bytes=64) for j in range(PAIRS)]
+        ca = [keep.tile([P, 2 * P], U32, name="ca%d" % j, align_bytes=64) for j in range(PAIRS)]
+        so = [keep.tile([P, 2 * P], U8, name="so%d" % j, align_bytes=64) for j in range(PAIRS)]
+        sa = [keep.tile([P, 2 * P], U8, name="sa%d" % j, align_bytes=64) for j in range(PAIRS)]
+        u_sb = [keep.tile([P, D], F32, name="u_sb%d" % b) for b in range(B)]
+        t_sb = [keep.tile([P, D], F32, name="t_sb%d" % b) for b in range(B)]
+        aT_sb = keep.tile([P, P], BF16, name="aT_sb")
+        b_bc = keep.tile([P, D], F32, name="b_bc")
+        m_bc = keep.tile([P, D], F32, name="m_bc")
+        o_ps = {}
+        g_ps = {}
+
+        def front_o(j):
+            if not 0 <= j < PAIRS:
+                return
+            oT_ps = psum.tile([P, 2, 2, P], F32, name="oT_ps%d" % j, tag="oT%d" % (j % 2))
+            words = o_sb[j][:].bitcast(F32)
+            for s in range(2):
+                for u in range(2):
+                    c0 = 256 * s + P * u
+                    nc.tensor.transpose(oT_ps[:, s, u, :], words[:, c0 : c0 + P], ident_f[:])
+            nc.scalar.copy(
+                out=go[j][:].bitcast(F32).rearrange("p (s i u) -> p s i u", s=2, u=2),
+                in_=oT_ps[:].rearrange("p s u i -> p s i u"),
+            )
+
+        def front_a(j):
+            if not 0 <= j < PAIRS:
+                return
+            banks = []
+            for s in range(2):
+                agg_ps = psum.tile([P, 4, P], F32, name="agg_ps%d" % (2 * j + s), tag="ag%d" % s)
+                for t in range(4):
+                    nc.tensor.matmul(
+                        agg_ps[:, t, :],
+                        lhsT=h_sb[j][:, s, P * t : P * t + P],
+                        rhs=aT_sb[:],
+                        start=True,
+                        stop=True,
+                    )
+                banks.append(agg_ps)
+            for s in range(2):
+                nc.scalar.copy(
+                    out=ga[j][:, D * s : D * s + D].rearrange("p (i t) -> p i t", t=4),
+                    in_=banks[s][:].rearrange("p t i -> p i t"),
+                )
+
+        def quant_o(j):
+            if 0 <= j < PAIRS:
+                quantise(co[j][:], so[j][:], go[j][:])
+
+        def quant_a(j):
+            if 0 <= j < PAIRS:
+                quantise(ca[j][:], sa[j][:], ga[j][:])
+
+        def mx(bank, codes, scales, s, w_codes, w_scales):
+            nc.tensor.matmul_mx(
+                out=bank[:],
+                lhsT=codes[:, P * s : P * s + P].bitcast(FP8X4),
+                lhsT_scale=scales[:, P * s : P * s + P],
+                rhs=w_codes[:].bitcast(FP8X4),
+                rhs_scale=w_scales[:],
+                start=True,
+                stop=True,
+            )
+
+        def mx_o(j):
+            if not 0 <= j < PAIRS:
+                return
+            for s in range(2):
+                bank = psum.tile([P, D], F32, name="o_ps%d" % (2 * j + s), tag="O%d" % s)
+                mx(bank, co[j], so[j], s, wp_codes, wp_scales)
+                o_ps[2 * j + s] = bank
+
+        def mx_g(j):
+            if not 0 <= j < PAIRS:
+                return
+            for s in range(2):
+                bank = psum.tile([P, D], F32, name="g_ps%d" % (2 * j + s), tag="G%d" % s)
+                mx(bank, ca[j], sa[j], s, gw_codes, gw_scales)
+                g_ps[2 * j + s] = bank
+
+        def bias(b):
+            if 0 <= b < B:
+                nc.vector.tensor_tensor(out=u_sb[b][:], in0=o_ps[b][:], in1=b_bc[:], op=ADD)
+
+        def gain_add_store(b):
+            if not 0 <= b < B:
+                return
+            nc.vector.tensor_tensor(out=t_sb[b][:], in0=g_ps[b][:], in1=m_bc[:], op=MULT)
+            adder = nc.vector if b in VECTOR_ADDS else nc.gpsimd
+            adder.tensor_tensor(out=u_sb[b][:], in0=u_sb[b][:], in1=t_sb[b][:], op=ADD)
+            nc.sync.dma_start(out=out[b], in_=u_sb[b][:])
+
+        regroup(nc.scalar.copy, wp_grp, wp_raw, 0, WP_S_COLS)
+        regroup(nc.vector.tensor_copy, wp_grp, wp_raw, WP_S_COLS, D)
+        quantise(wp_codes[:], wp_scales[:], wp_grp[:].rearrange("p c t -> p (c t)"))
+
+        aT_ps = psum.tile([P, P], BF16, name="aT_ps", tag="ag0")
+        nc.tensor.transpose(aT_ps[:], a_sb[:], ident_bf[:])
+        nc.scalar.copy(out=aT_sb[:], in_=aT_ps[:])
+
+        front_o(0)
+
+        b_ps = psum.tile([P, D], F32, name="b_ps", tag="G0")
+        m_ps = psum.tile([P, D], F32, name="m_ps", tag="G1")
+        nc.tensor.matmul(b_ps[:], lhsT=ones[:], rhs=rows[:, 0:D], start=True, stop=True)
+        nc.tensor.matmul(m_ps[:], lhsT=ones[:], rhs=rows[:, D : 2 * D], start=True, stop=True)
+        nc.scalar.copy(out=b_bc[:], in_=b_ps[:])
+
+        for j in range(-2, PAIRS):
+            if j == -2:
+                regroup(nc.scalar.copy, gw_grp, gw_raw, 0, GW_S_COLS)
+                nc.scalar.copy(out=m_bc[:], in_=m_ps[:])
+            front_o(j + 3)
+            front_a(j + 2)
+            gain_add_store(2 * j)
+            quant_o(j + 2)
+            mx_o(j + 2)
+            if j == -2:
+                regroup(nc.vector.tensor_copy, gw_grp, gw_raw, GW_S_COLS, D)
+                quantise(gw_codes[:], gw_scales[:], gw_grp[:].rearrange("p c t -> p (c t)"))
+            gain_add_store(2 * j + 1)
+            quant_a(j + 1)
+            mx_g(j + 1)
+            bias(2 * j + 4)
+            bias(2 * j + 5)

@@ -17,10 +17,6 @@ D = 512
 PAIRS = B // 2
 FLOPS = 2 * B * P * D * D * 2 + 2 * B * P * P * D
 
-WP_S_COLS = 160
-GW_S_COLS = 128
-VECTOR_ADDS = (11,)
-
 
 def tile_gatblock_pa_kernel(tc, h_norm, o_attn, a_gcn, w_proj, b_proj, gcn_w, gcn_m, out):
     nc = tc.nc
@@ -33,16 +29,25 @@ def tile_gatblock_pa_kernel(tc, h_norm, o_attn, a_gcn, w_proj, b_proj, gcn_w, gc
         ones = keep.tile([P, P], BF16, name="ones")
         ident_bf = keep.tile([P, P], BF16, name="ident_bf")
         ident_f = keep.tile([P, P], F32, name="ident_f")
-        nc.vector.memset(rows[:], 0.0)
-        nc.vector.memset(ones[:], 1.0)
-        make_identity(nc, ident_f[:])
-        make_identity(nc, ident_bf[:])
-
         wp_raw = keep.tile([P, 4, D], BF16, name="wp_raw")
         gw_raw = keep.tile([P, 4, D], BF16, name="gw_raw")
         a_sb = keep.tile([P, P], BF16, name="a_sb")
         o_sb = [keep.tile([P, 2 * D], BF16, name="o_sb%d" % j) for j in range(PAIRS)]
         h_sb = [keep.tile([P, 2, D], BF16, name="h_sb%d" % j) for j in range(PAIRS)]
+        wp_grp = keep.tile([P, D, 4], BF16, name="wp_grp", align_bytes=64)
+        gw_grp = keep.tile([P, D, 4], BF16, name="gw_grp", align_bytes=64)
+        wp_codes = keep.tile([P, D], U32, name="wp_codes", align_bytes=64)
+        gw_codes = keep.tile([P, D], U32, name="gw_codes", align_bytes=64)
+        wp_scales = keep.tile([P, D], U8, name="wp_scales", align_bytes=64)
+        gw_scales = keep.tile([P, D], U8, name="gw_scales", align_bytes=64)
+        grouped = keep.tile([P, 2, B * D], BF16, name="grouped", align_bytes=64)
+        codes = keep.tile([P, 2, B * P], U32, name="codes", align_bytes=64)
+        scales = keep.tile([P, 2, B * P], U8, name="scales", align_bytes=64)
+        u_sb = [keep.tile([P, D], F32, name="u_sb%d" % b) for b in range(B)]
+        t_sb = [keep.tile([P, D], F32, name="t_sb%d" % b) for b in range(B)]
+        aT_sb = keep.tile([P, P], BF16, name="aT_sb")
+        bm_bc = keep.tile([P, 2 * D], BF16, name="bm_bc")
+        bank = {}
 
         def load_o(j):
             nc.sync.dma_start(
@@ -53,19 +58,14 @@ def tile_gatblock_pa_kernel(tc, h_norm, o_attn, a_gcn, w_proj, b_proj, gcn_w, gc
         def load_h(j):
             nc.sync.dma_start(out=h_sb[j][:], in_=h_norm[2 * j : 2 * j + 2].rearrange("s n d -> n s d"))
 
-        nc.sync.dma_start(
-            out=wp_raw[:].rearrange("p (u e) c -> p u e c", u=2),
-            in_=w_proj.rearrange("(u p e) c -> p u e c", u=2, p=P, e=2),
-        )
-        nc.scalar.dma_start(out=a_sb[:], in_=a_gcn)
-        nc.scalar.dma_start(out=rows[0:1, 0:D], in_=b_proj.rearrange("(o n) -> o n", o=1))
-        nc.scalar.dma_start(out=rows[0:1, D : 2 * D], in_=gcn_m.rearrange("(o n) -> o n", o=1))
-        load_o(0)
-        nc.sync.dma_start(out=gw_raw[:], in_=gcn_w.rearrange("(t p) c -> p t c", t=4, p=P))
-        load_h(0)
-        for j in range(1, PAIRS):
-            load_o(j)
-            load_h(j)
+        def load_wp():
+            nc.sync.dma_start(
+                out=wp_raw[:].rearrange("p (u e) c -> p u e c", u=2),
+                in_=w_proj.rearrange("(u p e) c -> p u e c", u=2, p=P, e=2),
+            )
+
+        def load_gw():
+            nc.sync.dma_start(out=gw_raw[:], in_=gcn_w.rearrange("(t p) c -> p t c", t=4, p=P))
 
         def regroup(engine_copy, grp, raw, c0, c1):
             engine_copy(
@@ -73,142 +73,245 @@ def tile_gatblock_pa_kernel(tc, h_norm, o_attn, a_gcn, w_proj, b_proj, gcn_w, gc
                 in_=raw[:, :, c0:c1].rearrange("p t (c i) -> p c t i", i=4),
             )
 
-        wp_grp = keep.tile([P, D, 4], BF16, name="wp_grp", align_bytes=64)
-        gw_grp = keep.tile([P, D, 4], BF16, name="gw_grp", align_bytes=64)
-        wp_codes = keep.tile([P, D], U32, name="wp_codes", align_bytes=64)
-        gw_codes = keep.tile([P, D], U32, name="gw_codes", align_bytes=64)
-        wp_scales = keep.tile([P, D], U8, name="wp_scales", align_bytes=64)
-        gw_scales = keep.tile([P, D], U8, name="gw_scales", align_bytes=64)
+        def quantise_w(w_codes, w_scales, grp):
+            nc.vector.quantize_mx(
+                out=w_codes[:].bitcast(FP8X4), scales=w_scales[:], in_=grp[:].rearrange("p c t -> p (c t)")
+            )
 
-        def quantise(codes, scales, grouped):
-            nc.vector.quantize_mx(out=codes.bitcast(FP8X4), scales=scales, in_=grouped)
+        def quantise(branch, b0, n):
+            nc.vector.quantize_mx(
+                out=codes[:, branch, P * b0 : P * (b0 + n)].bitcast(FP8X4),
+                scales=scales[:, branch, P * b0 : P * (b0 + n)],
+                in_=grouped[:, branch, D * b0 : D * (b0 + n)],
+            )
 
-        go = [keep.tile([P, 2 * D], BF16, name="go%d" % j, align_bytes=64) for j in range(PAIRS)]
-        ga = [keep.tile([P, 2 * D], BF16, name="ga%d" % j, align_bytes=64) for j in range(PAIRS)]
-        co = [keep.tile([P, 2 * P], U32, name="co%d" % j, align_bytes=64) for j in range(PAIRS)]
-        ca = [keep.tile([P, 2 * P], U32, name="ca%d" % j, align_bytes=64) for j in range(PAIRS)]
-        so = [keep.tile([P, 2 * P], U8, name="so%d" % j, align_bytes=64) for j in range(PAIRS)]
-        sa = [keep.tile([P, 2 * P], U8, name="sa%d" % j, align_bytes=64) for j in range(PAIRS)]
-        u_sb = [keep.tile([P, D], F32, name="u_sb%d" % b) for b in range(B)]
-        t_sb = [keep.tile([P, D], F32, name="t_sb%d" % b) for b in range(B)]
-        aT_sb = keep.tile([P, P], BF16, name="aT_sb")
-        b_bc = keep.tile([P, D], F32, name="b_bc")
-        m_bc = keep.tile([P, D], F32, name="m_bc")
-        o_ps = {}
-        g_ps = {}
+        def a_transpose(tag):
+            bank["aT"] = psum.tile([P, P], BF16, name="aT_ps", tag=tag)
+            nc.tensor.transpose(bank["aT"][:], a_sb[:], ident_bf[:])
 
-        def front_o(j):
-            if not 0 <= j < PAIRS:
-                return
-            oT_ps = psum.tile([P, 2, 2, P], F32, name="oT_ps%d" % j, tag="oT%d" % (j % 2))
+        def spread_bm(tag):
+            bank["bm"] = psum.tile([P, 2 * D], BF16, name="bm_ps", tag=tag)
+            for half in range(2):
+                nc.tensor.matmul(
+                    bank["bm"][:, D * half : D * half + D],
+                    lhsT=ones[:],
+                    rhs=rows[:, D * half : D * half + D],
+                    start=True,
+                    stop=True,
+                )
+
+        def front_t(j, tag):
+            oT_ps = psum.tile([P, 2, 2, P], F32, name="oT_ps%d" % j, tag=tag)
             words = o_sb[j][:].bitcast(F32)
             for s in range(2):
                 for u in range(2):
                     c0 = 256 * s + P * u
                     nc.tensor.transpose(oT_ps[:, s, u, :], words[:, c0 : c0 + P], ident_f[:])
-            nc.scalar.copy(
-                out=go[j][:].bitcast(F32).rearrange("p (s i u) -> p s i u", s=2, u=2),
-                in_=oT_ps[:].rearrange("p s u i -> p s i u"),
+            bank["oT", j] = oT_ps
+
+        def exit_o(engine_copy, j):
+            engine_copy(
+                out=grouped[:, 0, 2 * D * j : 2 * D * (j + 1)].bitcast(F32).rearrange("p (s i u) -> p s i u", s=2, u=2),
+                in_=bank["oT", j][:].rearrange("p s u i -> p s i u"),
             )
 
-        def front_a(j):
-            if not 0 <= j < PAIRS:
-                return
-            banks = []
-            for s in range(2):
-                agg_ps = psum.tile([P, 4, P], F32, name="agg_ps%d" % (2 * j + s), tag="ag%d" % s)
-                for t in range(4):
-                    nc.tensor.matmul(
-                        agg_ps[:, t, :],
-                        lhsT=h_sb[j][:, s, P * t : P * t + P],
-                        rhs=aT_sb[:],
-                        start=True,
-                        stop=True,
-                    )
-                banks.append(agg_ps)
-            for s in range(2):
-                nc.scalar.copy(
-                    out=ga[j][:, D * s : D * s + D].rearrange("p (i t) -> p i t", t=4),
-                    in_=banks[s][:].rearrange("p t i -> p i t"),
+        def front_a(b, tag):
+            agg_ps = psum.tile([P, 4, P], F32, name="agg_ps%d" % b, tag=tag)
+            for t in range(4):
+                nc.tensor.matmul(
+                    agg_ps[:, t, :],
+                    lhsT=h_sb[b // 2][:, b % 2, P * t : P * t + P],
+                    rhs=aT_sb[:],
+                    start=True,
+                    stop=True,
                 )
+            bank["ag", b] = agg_ps
 
-        def quant_o(j):
-            if 0 <= j < PAIRS:
-                quantise(co[j][:], so[j][:], go[j][:])
+        def exit_a(engine_copy, b):
+            engine_copy(
+                out=grouped[:, 1, D * b : D * (b + 1)].rearrange("p (i t) -> p i t", t=4),
+                in_=bank["ag", b][:].rearrange("p t i -> p i t"),
+            )
 
-        def quant_a(j):
-            if 0 <= j < PAIRS:
-                quantise(ca[j][:], sa[j][:], ga[j][:])
-
-        def mx(bank, codes, scales, s, w_codes, w_scales):
+        def mx(kind, branch, b, tag, w_codes, w_scales):
+            acc = psum.tile([P, D], F32, name="%s_ps%d" % (kind, b), tag=tag)
             nc.tensor.matmul_mx(
-                out=bank[:],
-                lhsT=codes[:, P * s : P * s + P].bitcast(FP8X4),
-                lhsT_scale=scales[:, P * s : P * s + P],
+                out=acc[:],
+                lhsT=codes[:, branch, P * b : P * b + P].bitcast(FP8X4),
+                lhsT_scale=scales[:, branch, P * b : P * b + P],
                 rhs=w_codes[:].bitcast(FP8X4),
                 rhs_scale=w_scales[:],
                 start=True,
                 stop=True,
             )
+            bank[kind, b] = acc
 
-        def mx_o(j):
-            if not 0 <= j < PAIRS:
-                return
-            for s in range(2):
-                bank = psum.tile([P, D], F32, name="o_ps%d" % (2 * j + s), tag="O%d" % s)
-                mx(bank, co[j], so[j], s, wp_codes, wp_scales)
-                o_ps[2 * j + s] = bank
+        def mx_o(b, tag):
+            mx("o", 0, b, tag, wp_codes, wp_scales)
 
-        def mx_g(j):
-            if not 0 <= j < PAIRS:
-                return
-            for s in range(2):
-                bank = psum.tile([P, D], F32, name="g_ps%d" % (2 * j + s), tag="G%d" % s)
-                mx(bank, ca[j], sa[j], s, gw_codes, gw_scales)
-                g_ps[2 * j + s] = bank
+        def mx_g(b, tag):
+            mx("g", 1, b, tag, gw_codes, gw_scales)
 
         def bias(b):
-            if 0 <= b < B:
-                nc.vector.tensor_tensor(out=u_sb[b][:], in0=o_ps[b][:], in1=b_bc[:], op=ADD)
+            nc.vector.tensor_tensor(out=u_sb[b][:], in0=bank["o", b][:], in1=bm_bc[:, 0:D], op=ADD)
 
-        def gain_add_store(b):
-            if not 0 <= b < B:
-                return
-            nc.vector.tensor_tensor(out=t_sb[b][:], in0=g_ps[b][:], in1=m_bc[:], op=MULT)
-            adder = nc.vector if b in VECTOR_ADDS else nc.gpsimd
-            adder.tensor_tensor(out=u_sb[b][:], in0=u_sb[b][:], in1=t_sb[b][:], op=ADD)
+        def gain(b):
+            nc.vector.tensor_tensor(out=t_sb[b][:], in0=bank["g", b][:], in1=bm_bc[:, D : 2 * D], op=MULT)
+
+        def join(engine, b):
+            engine.tensor_tensor(out=u_sb[b][:], in0=u_sb[b][:], in1=t_sb[b][:], op=ADD)
+
+        def store(b):
             nc.sync.dma_start(out=out[b], in_=u_sb[b][:])
 
-        regroup(nc.scalar.copy, wp_grp, wp_raw, 0, WP_S_COLS)
-        regroup(nc.vector.tensor_copy, wp_grp, wp_raw, WP_S_COLS, D)
-        quantise(wp_codes[:], wp_scales[:], wp_grp[:].rearrange("p c t -> p (c t)"))
-
-        aT_ps = psum.tile([P, P], BF16, name="aT_ps", tag="ag0")
-        nc.tensor.transpose(aT_ps[:], a_sb[:], ident_bf[:])
-        nc.scalar.copy(out=aT_sb[:], in_=aT_ps[:])
-
-        front_o(0)
-
-        b_ps = psum.tile([P, D], F32, name="b_ps", tag="G0")
-        m_ps = psum.tile([P, D], F32, name="m_ps", tag="G1")
-        nc.tensor.matmul(b_ps[:], lhsT=ones[:], rhs=rows[:, 0:D], start=True, stop=True)
-        nc.tensor.matmul(m_ps[:], lhsT=ones[:], rhs=rows[:, D : 2 * D], start=True, stop=True)
-        nc.scalar.copy(out=b_bc[:], in_=b_ps[:])
-
-        for j in range(-2, PAIRS):
-            if j == -2:
-                regroup(nc.scalar.copy, gw_grp, gw_raw, 0, GW_S_COLS)
-                nc.scalar.copy(out=m_bc[:], in_=m_ps[:])
-            front_o(j + 3)
-            front_a(j + 2)
-            gain_add_store(2 * j)
-            quant_o(j + 2)
-            mx_o(j + 2)
-            if j == -2:
-                regroup(nc.vector.tensor_copy, gw_grp, gw_raw, GW_S_COLS, D)
-                quantise(gw_codes[:], gw_scales[:], gw_grp[:].rearrange("p c t -> p (c t)"))
-            gain_add_store(2 * j + 1)
-            quant_a(j + 1)
-            mx_g(j + 1)
-            bias(2 * j + 4)
-            bias(2 * j + 5)
+        nc.vector.memset(rows[:], 0.0)
+        make_identity(nc, ident_f[:])
+        load_wp()
+        nc.scalar.dma_start(out=a_sb[:], in_=a_gcn)
+        load_o(0)
+        load_gw()
+        nc.vector.memset(ones[:], 1.0)
+        load_h(0)
+        load_o(1)
+        nc.scalar.dma_start(out=rows[0:1, 0:D], in_=b_proj.rearrange("(o n) -> o n", o=1))
+        make_identity(nc, ident_bf[:])
+        nc.scalar.dma_start(out=rows[0:1, D : 2 * D], in_=gcn_m.rearrange("(o n) -> o n", o=1))
+        a_transpose("ag0")
+        nc.scalar.copy(out=aT_sb[:], in_=bank["aT"][:])
+        load_h(1)
+        regroup(nc.vector.tensor_copy, wp_grp, wp_raw, 160, D)
+        regroup(nc.scalar.copy, wp_grp, wp_raw, 0, 160)
+        load_o(2)
+        load_h(2)
+        spread_bm("G0")
+        load_o(3)
+        load_h(3)
+        front_t(0, "oT0")
+        quantise_w(wp_codes, wp_scales, wp_grp)
+        nc.scalar.copy(out=bm_bc[:], in_=bank["bm"][:])
+        exit_o(nc.scalar.copy, 0)
+        load_o(4)
+        regroup(nc.vector.tensor_copy, gw_grp, gw_raw, 128, D)
+        regroup(nc.scalar.copy, gw_grp, gw_raw, 0, 128)
+        load_h(4)
+        front_a(0, "ag1")
+        quantise(0, 0, 2)
+        front_a(1, "ag0")
+        quantise_w(gw_codes, gw_scales, gw_grp)
+        exit_a(nc.scalar.copy, 0)
+        load_o(5)
+        front_t(1, "oT1")
+        mx_o(0, "O0")
+        exit_a(nc.scalar.copy, 1)
+        load_h(5)
+        mx_o(1, "O1")
+        exit_o(nc.scalar.copy, 1)
+        bias(0)
+        front_a(2, "ag1")
+        front_a(3, "ag0")
+        exit_a(nc.scalar.copy, 2)
+        quantise(1, 0, 2)
+        front_t(2, "oT0")
+        quantise(0, 2, 2)
+        mx_g(0, "G1")
+        exit_a(nc.scalar.copy, 3)
+        bias(1)
+        mx_g(1, "G0")
+        exit_o(nc.scalar.copy, 2)
+        gain(0)
+        mx_o(2, "O0")
+        mx_o(3, "O1")
+        quantise(1, 2, 2)
+        front_a(4, "ag1")
+        quantise(0, 4, 2)
+        front_a(5, "ag0")
+        exit_a(nc.scalar.copy, 4)
+        mx_g(2, "G1")
+        gain(1)
+        join(nc.gpsimd, 0)
+        front_t(3, "oT1")
+        exit_a(nc.scalar.copy, 5)
+        bias(2)
+        front_t(4, "oT0")
+        mx_g(3, "G0")
+        exit_o(nc.scalar.copy, 3)
+        gain(2)
+        join(nc.gpsimd, 1)
+        mx_o(4, "O0")
+        store(0)
+        exit_o(nc.scalar.copy, 4)
+        bias(3)
+        front_a(6, "ag1")
+        front_a(7, "ag0")
+        gain(3)
+        exit_a(nc.scalar.copy, 6)
+        front_t(5, "oT1")
+        join(nc.gpsimd, 2)
+        mx_o(5, "O1")
+        store(1)
+        bias(4)
+        exit_a(nc.scalar.copy, 7)
+        front_a(8, "ag1")
+        bias(5)
+        exit_o(nc.scalar.copy, 5)
+        join(nc.gpsimd, 3)
+        front_a(9, "ag0")
+        store(2)
+        exit_a(nc.scalar.copy, 8)
+        exit_a(nc.scalar.copy, 9)
+        front_a(10, "ag1")
+        quantise(1, 4, 2)
+        store(3)
+        quantise(0, 6, 2)
+        exit_a(nc.scalar.copy, 10)
+        front_a(11, "ag0")
+        quantise(1, 6, 2)
+        mx_g(4, "G1")
+        quantise(0, 8, 2)
+        exit_a(nc.scalar.copy, 11)
+        mx_g(5, "G0")
+        quantise(1, 8, 2)
+        mx_o(6, "O0")
+        quantise(0, 10, 2)
+        mx_o(7, "O1")
+        gain(4)
+        quantise(1, 10, 2)
+        mx_g(6, "G1")
+        gain(5)
+        join(nc.gpsimd, 4)
+        bias(6)
+        mx_g(7, "G0")
+        gain(6)
+        join(nc.gpsimd, 5)
+        mx_o(8, "O0")
+        store(4)
+        bias(7)
+        mx_g(8, "G1")
+        gain(7)
+        join(nc.gpsimd, 6)
+        mx_o(9, "O1")
+        store(5)
+        bias(8)
+        mx_g(9, "G0")
+        gain(8)
+        join(nc.gpsimd, 7)
+        mx_o(10, "O0")
+        store(6)
+        bias(9)
+        mx_g(10, "G1")
+        gain(9)
+        mx_o(11, "O1")
+        join(nc.gpsimd, 8)
+        store(7)
+        bias(10)
+        mx_g(11, "G0")
+        gain(10)
+        join(nc.gpsimd, 9)
+        bias(11)
+        store(8)
+        gain(11)
+        join(nc.vector, 10)
+        store(9)
+        join(nc.vector, 11)
+        store(10)
+        store(11)

@@ -40,13 +40,18 @@ def tile_gatblock_pa_kernel(tc, h_norm, o_attn, a_gcn, w_proj, b_proj, gcn_w, gc
         gw_codes = keep.tile([P, D], U32, name="gw_codes", align_bytes=64)
         wp_scales = keep.tile([P, D], U8, name="wp_scales", align_bytes=64)
         gw_scales = keep.tile([P, D], U8, name="gw_scales", align_bytes=64)
-        grouped = keep.tile([P, 2, B * D], BF16, name="grouped", align_bytes=64)
-        codes = keep.tile([P, 2, B * P], U32, name="codes", align_bytes=64)
-        scales = keep.tile([P, 2, B * P], U8, name="scales", align_bytes=64)
+        grouped = [[keep.tile([P, 2 * D], BF16, name="grouped%d_%d" % (k, j), align_bytes=64) for j in range(PAIRS)] for k in range(2)]
+        codes = [[keep.tile([P, 2 * P], U32, name="codes%d_%d" % (k, j), align_bytes=64) for j in range(PAIRS)] for k in range(2)]
+        scales = [[keep.tile([P, 2 * P], U8, name="scales%d_%d" % (k, j), align_bytes=64) for j in range(PAIRS)] for k in range(2)]
         u_sb = [keep.tile([P, D], F32, name="u_sb%d" % b) for b in range(B)]
         t_sb = [keep.tile([P, D], F32, name="t_sb%d" % b) for b in range(B)]
         aT_sb = keep.tile([P, P], BF16, name="aT_sb")
         bm_bc = keep.tile([P, 2 * D], BF16, name="bm_bc")
+        cols_in = keep.tile([P, P], BF16, name="cols_in")
+        col_sb = keep.tile([P, 8], F32, name="col_sb")
+        warm = keep.tile([P, 1], F32, name="warm")
+        tT = {}
+        ox = {}
         bank = {}
 
         def load_o(j):
@@ -79,11 +84,9 @@ def tile_gatblock_pa_kernel(tc, h_norm, o_attn, a_gcn, w_proj, b_proj, gcn_w, gc
             )
 
         def quantise(branch, b0, n):
-            nc.vector.quantize_mx(
-                out=codes[:, branch, P * b0 : P * (b0 + n)].bitcast(FP8X4),
-                scales=scales[:, branch, P * b0 : P * (b0 + n)],
-                in_=grouped[:, branch, D * b0 : D * (b0 + n)],
-            )
+            assert n == 2
+            j = b0 // 2
+            nc.vector.quantize_mx(out=codes[branch][j][:].bitcast(FP8X4), scales=scales[branch][j][:], in_=grouped[branch][j][:])
 
         def a_transpose(tag):
             bank["aT"] = psum.tile([P, P], BF16, name="aT_ps", tag=tag)
@@ -111,7 +114,7 @@ def tile_gatblock_pa_kernel(tc, h_norm, o_attn, a_gcn, w_proj, b_proj, gcn_w, gc
 
         def exit_o(engine_copy, j):
             engine_copy(
-                out=grouped[:, 0, 2 * D * j : 2 * D * (j + 1)].bitcast(F32).rearrange("p (s i u) -> p s i u", s=2, u=2),
+                out=grouped[0][j][:].bitcast(F32).rearrange("p (s i u) -> p s i u", s=2, u=2),
                 in_=bank["oT", j][:].rearrange("p s u i -> p s i u"),
             )
 
@@ -129,7 +132,7 @@ def tile_gatblock_pa_kernel(tc, h_norm, o_attn, a_gcn, w_proj, b_proj, gcn_w, gc
 
         def exit_a(engine_copy, b):
             engine_copy(
-                out=grouped[:, 1, D * b : D * (b + 1)].rearrange("p (i t) -> p i t", t=4),
+                out=grouped[1][b // 2][:, D * (b % 2) : D * (b % 2 + 1)].rearrange("p (i t) -> p i t", t=4),
                 in_=bank["ag", b][:].rearrange("p t i -> p i t"),
             )
 
@@ -137,8 +140,8 @@ def tile_gatblock_pa_kernel(tc, h_norm, o_attn, a_gcn, w_proj, b_proj, gcn_w, gc
             acc = psum.tile([P, D], F32, name="%s_ps%d" % (kind, b), tag=tag)
             nc.tensor.matmul_mx(
                 out=acc[:],
-                lhsT=codes[:, branch, P * b : P * b + P].bitcast(FP8X4),
-                lhsT_scale=scales[:, branch, P * b : P * b + P],
+                lhsT=codes[branch][b // 2][:, P * (b % 2) : P * (b % 2) + P].bitcast(FP8X4),
+                lhsT_scale=scales[branch][b // 2][:, P * (b % 2) : P * (b % 2) + P],
                 rhs=w_codes[:].bitcast(FP8X4),
                 rhs_scale=w_scales[:],
                 start=True,
@@ -161,6 +164,50 @@ def tile_gatblock_pa_kernel(tc, h_norm, o_attn, a_gcn, w_proj, b_proj, gcn_w, gc
         def join(engine, b):
             engine.tensor_tensor(out=u_sb[b][:], in0=u_sb[b][:], in1=t_sb[b][:], op=ADD)
 
+        def load_cols(half, vec):
+            nc.sync.dma_start(out=cols_in[4 * half : 4 * half + 4, :], in_=vec.rearrange("(c p) -> c p", p=P))
+
+        def cols_transpose(tag):
+            bank["col"] = psum.tile([P, P], BF16, name="col_ps", tag=tag)
+            nc.tensor.transpose(bank["col"][:], cols_in[:], ident_bf[:])
+
+        def mx_gt(j, c, tag):
+            if c % 2 == 0:
+                bank["gt", j, c // 2] = psum.tile([P, 2, 2 * P], F32, name="gt_ps%d_%d" % (j, c // 2), tag=tag)
+            nc.tensor.matmul_mx(
+                out=bank["gt", j, c // 2][:, c % 2, :],
+                lhsT=gw_codes[:, P * c : P * c + P].bitcast(FP8X4),
+                lhsT_scale=gw_scales[:, P * c : P * c + P],
+                rhs=codes[1][j][:].bitcast(FP8X4),
+                rhs_scale=scales[1][j][:],
+                start=True,
+                stop=True,
+            )
+
+        def gain_bias_t(j, c):
+            if j not in tT:
+                tT[j] = keep.tile([P, 4, 2 * P], F32, name="tT%d" % j)
+            nc.scalar.activation(
+                out=tT[j][:, c, :],
+                in_=bank["gt", j, c // 2][:, c % 2, :],
+                func=mybir.ActivationFunctionType.Identity,
+                bias=col_sb[:, c : c + 1],
+                scale=col_sb[:, 4 + c : 5 + c],
+            )
+
+        def back_t(b, tag):
+            x_ps = psum.tile([P, D], F32, name="x_ps%d" % b, tag=tag)
+            for c in range(4):
+                nc.tensor.transpose(x_ps[:, P * c : P * c + P], tT[b // 2][:, c, P * (b % 2) : P * (b % 2) + P], ident_f[:])
+            bank["x", b] = x_ps
+
+        def exit_proj(engine_copy, b):
+            ox[b] = keep.tile([P, D], F32, name="ox%d" % b)
+            engine_copy(out=ox[b][:], in_=bank["o", b][:])
+
+        def join_t(b):
+            nc.vector.tensor_tensor(out=u_sb[b][:], in0=bank["x", b][:], in1=ox[b][:], op=ADD)
+
         def store(b):
             nc.sync.dma_start(out=out[b], in_=u_sb[b][:])
 
@@ -170,148 +217,166 @@ def tile_gatblock_pa_kernel(tc, h_norm, o_attn, a_gcn, w_proj, b_proj, gcn_w, gc
         nc.scalar.dma_start(out=a_sb[:], in_=a_gcn)
         load_o(0)
         load_gw()
-        nc.vector.memset(ones[:], 1.0)
         load_h(0)
         load_o(1)
         nc.scalar.dma_start(out=rows[0:1, 0:D], in_=b_proj.rearrange("(o n) -> o n", o=1))
         make_identity(nc, ident_bf[:])
         nc.scalar.dma_start(out=rows[0:1, D : 2 * D], in_=gcn_m.rearrange("(o n) -> o n", o=1))
-        a_transpose("ag0")
-        nc.scalar.copy(out=aT_sb[:], in_=bank["aT"][:])
-        load_h(1)
+        nc.scalar.activation(out=warm[:], in_=ident_f[:, 0:1], func=mybir.ActivationFunctionType.Identity)
+        a_transpose("F0")
         regroup(nc.vector.tensor_copy, wp_grp, wp_raw, 160, D)
+        load_h(1)
         regroup(nc.scalar.copy, wp_grp, wp_raw, 0, 160)
         load_o(2)
         load_h(2)
-        spread_bm("G0")
         load_o(3)
         load_h(3)
-        front_t(0, "oT0")
+        front_t(0, "F1")
+        nc.scalar.copy(out=aT_sb[:], in_=bank["aT"][:])
+        nc.vector.memset(ones[:], 1.0)
         quantise_w(wp_codes, wp_scales, wp_grp)
-        nc.scalar.copy(out=bm_bc[:], in_=bank["bm"][:])
+        spread_bm("G0")
         exit_o(nc.scalar.copy, 0)
         load_o(4)
-        regroup(nc.vector.tensor_copy, gw_grp, gw_raw, 128, D)
         regroup(nc.scalar.copy, gw_grp, gw_raw, 0, 128)
-        load_h(4)
-        front_a(0, "ag1")
         quantise(0, 0, 2)
-        front_a(1, "ag0")
-        quantise_w(gw_codes, gw_scales, gw_grp)
-        exit_a(nc.scalar.copy, 0)
-        load_o(5)
-        front_t(1, "oT1")
+        nc.vector.memset(cols_in[:], 0.0)
+        regroup(nc.vector.tensor_copy, gw_grp, gw_raw, 128, D)
+        nc.scalar.copy(out=bm_bc[:], in_=bank["bm"][:])
+        load_h(4)
+        front_a(0, "F2")
         mx_o(0, "O0")
+        exit_a(nc.scalar.copy, 0)
+        front_a(1, "F3")
+        quantise_w(gw_codes, gw_scales, gw_grp)
+        load_o(5)
+        front_t(1, "F0")
         exit_a(nc.scalar.copy, 1)
-        load_h(5)
         mx_o(1, "O1")
-        exit_o(nc.scalar.copy, 1)
         bias(0)
-        front_a(2, "ag1")
-        front_a(3, "ag0")
-        exit_a(nc.scalar.copy, 2)
+        load_h(5)
+        front_a(2, "F1")
+        exit_o(nc.scalar.copy, 1)
+        front_a(3, "F2")
         quantise(1, 0, 2)
-        front_t(2, "oT0")
+        load_cols(0, b_proj)
+        front_t(2, "F3")
+        exit_a(nc.scalar.copy, 2)
         quantise(0, 2, 2)
         mx_g(0, "G1")
-        exit_a(nc.scalar.copy, 3)
+        load_cols(1, gcn_m)
         bias(1)
-        mx_g(1, "G0")
+        exit_a(nc.scalar.copy, 3)
+        front_a(4, "F0")
+        mx_o(2, "O0")
         exit_o(nc.scalar.copy, 2)
         gain(0)
-        mx_o(2, "O0")
+        mx_g(1, "G0")
         mx_o(3, "O1")
-        quantise(1, 2, 2)
-        front_a(4, "ag1")
-        quantise(0, 4, 2)
-        front_a(5, "ag0")
         exit_a(nc.scalar.copy, 4)
-        mx_g(2, "G1")
+        quantise(1, 2, 2)
+        front_a(5, "F1")
+        quantise(0, 4, 2)
+        front_t(3, "F2")
         gain(1)
         join(nc.gpsimd, 0)
-        front_t(3, "oT1")
         exit_a(nc.scalar.copy, 5)
+        front_a(7, "F3")
+        mx_g(2, "G1")
         bias(2)
-        front_t(4, "oT0")
-        mx_g(3, "G0")
         exit_o(nc.scalar.copy, 3)
+        front_a(6, "F0")
+        mx_g(3, "G0")
         gain(2)
-        join(nc.gpsimd, 1)
-        mx_o(4, "O0")
-        store(0)
-        exit_o(nc.scalar.copy, 4)
-        bias(3)
-        front_a(6, "ag1")
-        front_a(7, "ag0")
-        gain(3)
-        exit_a(nc.scalar.copy, 6)
-        front_t(5, "oT1")
-        join(nc.gpsimd, 2)
-        mx_o(5, "O1")
-        store(1)
-        bias(4)
         exit_a(nc.scalar.copy, 7)
-        front_a(8, "ag1")
-        bias(5)
-        exit_o(nc.scalar.copy, 5)
-        join(nc.gpsimd, 3)
-        front_a(9, "ag0")
-        store(2)
+        join(nc.gpsimd, 1)
+        front_t(4, "F1")
+        store(0)
+        gain(3)
+        cols_transpose("F2")
+        exit_a(nc.scalar.copy, 6)
+        mx_o(4, "O0")
+        front_a(8, "F3")
+        nc.scalar.copy(out=col_sb[:], in_=bank["col"][:, 0:8])
+        exit_o(nc.scalar.copy, 4)
+        join(nc.gpsimd, 2)
+        bias(4)
+        front_a(9, "F0")
+        store(1)
+        front_t(5, "F2")
         exit_a(nc.scalar.copy, 8)
+        bias(3)
+        front_a(10, "F1")
+        mx_o(5, "O0")
         exit_a(nc.scalar.copy, 9)
-        front_a(10, "ag1")
         quantise(1, 4, 2)
-        store(3)
+        front_a(11, "F3")
+        store(2)
         quantise(0, 6, 2)
-        exit_a(nc.scalar.copy, 10)
-        front_a(11, "ag0")
-        quantise(1, 6, 2)
+        exit_o(nc.scalar.copy, 5)
         mx_g(4, "G1")
         quantise(0, 8, 2)
-        exit_a(nc.scalar.copy, 11)
         mx_g(5, "G0")
         quantise(1, 8, 2)
-        mx_o(6, "O0")
+        exit_a(nc.scalar.copy, 10)
+        mx_o(8, "F0")
+        quantise(1, 6, 2)
+        mx_gt(4, 2, "F2")
         quantise(0, 10, 2)
-        mx_o(7, "O1")
+        exit_proj(nc.scalar.copy, 8)
         gain(4)
-        quantise(1, 10, 2)
-        mx_g(6, "G1")
+        join(nc.gpsimd, 3)
+        mx_o(9, "F1")
+        mx_o(6, "O1")
+        exit_proj(nc.scalar.copy, 9)
         gain(5)
+        mx_gt(4, 3, None)
+        mx_g(6, "G1")
+        gain_bias_t(4, 3)
+        bias(5)
         join(nc.gpsimd, 4)
-        bias(6)
         mx_g(7, "G0")
+        store(3)
+        gain_bias_t(4, 2)
+        mx_o(10, "F0")
         gain(6)
-        join(nc.gpsimd, 5)
-        mx_o(8, "O0")
-        store(4)
-        bias(7)
-        mx_g(8, "G1")
+        mx_gt(4, 0, "F1")
+        exit_a(nc.scalar.copy, 11)
+        mx_gt(4, 1, None)
+        mx_o(7, "O0")
         gain(7)
-        join(nc.gpsimd, 6)
-        mx_o(9, "O1")
+        join(nc.gpsimd, 5)
+        mx_o(11, "F2")
+        gain_bias_t(4, 0)
+        store(4)
+        bias(6)
+        gain_bias_t(4, 1)
+        exit_proj(nc.scalar.copy, 11)
+        quantise(1, 10, 2)
         store(5)
-        bias(8)
-        mx_g(9, "G0")
-        gain(8)
-        join(nc.gpsimd, 7)
-        mx_o(10, "O0")
+        exit_proj(nc.vector.tensor_copy, 10)
+        join(nc.gpsimd, 6)
+        mx_gt(5, 0, "F3")
+        mx_gt(5, 1, None)
+        mx_gt(5, 2, "F1")
+        bias(7)
+        mx_gt(5, 3, None)
+        gain_bias_t(5, 1)
+        back_t(8, "F2")
+        join(nc.vector, 7)
+        gain_bias_t(5, 0)
+        back_t(9, "F0")
         store(6)
-        bias(9)
-        mx_g(10, "G1")
-        gain(9)
-        mx_o(11, "O1")
-        join(nc.gpsimd, 8)
+        gain_bias_t(5, 2)
+        join_t(8)
         store(7)
-        bias(10)
-        mx_g(11, "G0")
-        gain(10)
-        join(nc.gpsimd, 9)
-        bias(11)
+        gain_bias_t(5, 3)
+        join_t(9)
         store(8)
-        gain(11)
-        join(nc.vector, 10)
+        back_t(10, "F3")
+        back_t(11, "F2")
         store(9)
-        join(nc.vector, 11)
+        join_t(10)
+        join_t(11)
         store(10)
         store(11)

@@ -10,49 +10,75 @@ U32 = mybir.dt.uint32
 U8 = mybir.dt.uint8
 ADD = mybir.AluOpType.add
 MULT = mybir.AluOpType.mult
+IDENTITY = mybir.ActivationFunctionType.Identity
 
 P = 128
-B = 12
 D = 512
+PACK = 4
+B = 12
 PAIRS = B // 2
-FLOPS = 2 * B * P * D * D * 2 + 2 * B * P * P * D
+CHUNKS = D // P
+NODE_MAJOR = 8
+FLOPS = 2 * 2 * B * P * D * D + 2 * B * P * P * D
+
+SCALAR_COLS = (160, 128)
+VECTOR_JOINS = (6, 7)
+BANKS = {"front": 4, "proj": 2, "gcn": 2}
 
 
 def tile_gatblock_pa_kernel(tc, h_norm, o_attn, a_gcn, w_proj, b_proj, gcn_w, gcn_m, out):
     nc = tc.nc
     with ExitStack() as ctx:
-        keep = ctx.enter_context(tc.tile_pool(name="keep", bufs=1))
+        sbuf = ctx.enter_context(tc.tile_pool(name="sbuf", bufs=1))
         psum = ctx.enter_context(tc.psum_pool(name="psum", bufs=1))
         ctx.enter_context(tc.manual_schedule())
 
-        rows = keep.tile([P, 2 * D], BF16, name="rows")
-        ones = keep.tile([P, P], BF16, name="ones")
-        ident_bf = keep.tile([P, P], BF16, name="ident_bf")
-        ident_f = keep.tile([P, P], F32, name="ident_f")
-        wp_raw = keep.tile([P, 4, D], BF16, name="wp_raw")
-        gw_raw = keep.tile([P, 4, D], BF16, name="gw_raw")
-        a_sb = keep.tile([P, P], BF16, name="a_sb")
-        o_sb = [keep.tile([P, 2 * D], BF16, name="o_sb%d" % j) for j in range(PAIRS)]
-        h_sb = [keep.tile([P, 2, D], BF16, name="h_sb%d" % j) for j in range(PAIRS)]
-        wp_grp = keep.tile([P, D, 4], BF16, name="wp_grp", align_bytes=64)
-        gw_grp = keep.tile([P, D, 4], BF16, name="gw_grp", align_bytes=64)
-        wp_codes = keep.tile([P, D], U32, name="wp_codes", align_bytes=64)
-        gw_codes = keep.tile([P, D], U32, name="gw_codes", align_bytes=64)
-        wp_scales = keep.tile([P, D], U8, name="wp_scales", align_bytes=64)
-        gw_scales = keep.tile([P, D], U8, name="gw_scales", align_bytes=64)
-        grouped = [[keep.tile([P, 2 * D], BF16, name="grouped%d_%d" % (k, j), align_bytes=64) for j in range(PAIRS)] for k in range(2)]
-        codes = [[keep.tile([P, 2 * P], U32, name="codes%d_%d" % (k, j), align_bytes=64) for j in range(PAIRS)] for k in range(2)]
-        scales = [[keep.tile([P, 2 * P], U8, name="scales%d_%d" % (k, j), align_bytes=64) for j in range(PAIRS)] for k in range(2)]
-        u_sb = [keep.tile([P, D], F32, name="u_sb%d" % b) for b in range(B)]
-        t_sb = [keep.tile([P, D], F32, name="t_sb%d" % b) for b in range(B)]
-        aT_sb = keep.tile([P, P], BF16, name="aT_sb")
-        bm_bc = keep.tile([P, 2 * D], BF16, name="bm_bc")
-        cols_in = keep.tile([P, P], BF16, name="cols_in")
-        col_sb = keep.tile([P, 8], F32, name="col_sb")
-        warm = keep.tile([P, 1], F32, name="warm")
-        tT = {}
-        ox = {}
+        ident_f = sbuf.tile([P, P], F32, name="ident_f")
+        ident_bf = sbuf.tile([P, P], BF16, name="ident_bf")
+        ones = sbuf.tile([P, P], BF16, name="ones")
+        rows = sbuf.tile([P, 2 * D], BF16, name="rows")
+        spread = sbuf.tile([P, 2 * D], BF16, name="spread")
+        chunk_rows = sbuf.tile([P, P], BF16, name="chunk_rows")
+        per_feature = sbuf.tile([P, 2 * CHUNKS], F32, name="per_feature")
+        warm = sbuf.tile([P, 1], F32, name="warm")
+        a_sb = sbuf.tile([P, P], BF16, name="a_sb")
+        aT_sb = sbuf.tile([P, P], BF16, name="aT_sb")
+        w_dram = (w_proj, gcn_w)
+        w_raw = [sbuf.tile([P, PACK, D], BF16, name="w_raw%d" % w) for w in range(2)]
+        w_grouped = [sbuf.tile([P, D, PACK], BF16, name="w_grouped%d" % w, align_bytes=64) for w in range(2)]
+        w_codes = [sbuf.tile([P, D], U32, name="w_codes%d" % w, align_bytes=64) for w in range(2)]
+        w_scales = [sbuf.tile([P, D], U8, name="w_scales%d" % w, align_bytes=64) for w in range(2)]
+        o_sb = [sbuf.tile([P, 2 * D], BF16, name="o_sb%d" % j) for j in range(PAIRS)]
+        h_sb = [sbuf.tile([P, 2, D], BF16, name="h_sb%d" % j) for j in range(PAIRS)]
+        grouped = [
+            [sbuf.tile([P, 2 * D], BF16, name="grouped%d_%d" % (k, j), align_bytes=64) for j in range(PAIRS)]
+            for k in range(2)
+        ]
+        codes = [
+            [sbuf.tile([P, 2 * P], U32, name="codes%d_%d" % (k, j), align_bytes=64) for j in range(PAIRS)]
+            for k in range(2)
+        ]
+        scales = [
+            [sbuf.tile([P, 2 * P], U8, name="scales%d_%d" % (k, j), align_bytes=64) for j in range(PAIRS)]
+            for k in range(2)
+        ]
+        result = [sbuf.tile([P, D], F32, name="result%d" % b) for b in range(B)]
+        other = [sbuf.tile([P, D], F32, name="other%d" % b) for b in range(B)]
+        scaled_t = {j: sbuf.tile([P, CHUNKS, 2 * P], F32, name="scaled_t%d" % j) for j in range(NODE_MAJOR // 2, PAIRS)}
         bank = {}
+        taken = {group: 0 for group in BANKS}
+
+        def new_bank(group, shape, dtype, name):
+            tag = "%s%d" % (group, taken[group] % BANKS[group])
+            taken[group] = taken[group] + 1
+            return psum.tile(shape, dtype, name=name, tag=tag)
+
+        def load_weight(w):
+            if w == 0:
+                view = w_dram[w].rearrange("(u p e) c -> p u e c", u=2, p=P, e=2)
+                nc.sync.dma_start(out=w_raw[w][:].rearrange("p (u e) c -> p u e c", u=2), in_=view)
+            else:
+                nc.sync.dma_start(out=w_raw[w][:], in_=w_dram[w].rearrange("(t p) c -> p t c", t=PACK, p=P))
 
         def load_o(j):
             nc.sync.dma_start(
@@ -63,320 +89,177 @@ def tile_gatblock_pa_kernel(tc, h_norm, o_attn, a_gcn, w_proj, b_proj, gcn_w, gc
         def load_h(j):
             nc.sync.dma_start(out=h_sb[j][:], in_=h_norm[2 * j : 2 * j + 2].rearrange("s n d -> n s d"))
 
-        def load_wp():
-            nc.sync.dma_start(
-                out=wp_raw[:].rearrange("p (u e) c -> p u e c", u=2),
-                in_=w_proj.rearrange("(u p e) c -> p u e c", u=2, p=P, e=2),
+        def store(b):
+            nc.sync.dma_start(out=out[b], in_=result[b][:])
+
+        def regroup(copy, w, c0, c1):
+            copy(
+                out=w_grouped[w][:, c0:c1, :].rearrange("p (c i) t -> p c t i", i=4),
+                in_=w_raw[w][:, :, c0:c1].rearrange("p t (c i) -> p c t i", i=4),
             )
 
-        def load_gw():
-            nc.sync.dma_start(out=gw_raw[:], in_=gcn_w.rearrange("(t p) c -> p t c", t=4, p=P))
-
-        def regroup(engine_copy, grp, raw, c0, c1):
-            engine_copy(
-                out=grp[:, c0:c1, :].rearrange("p (c i) t -> p c t i", i=4),
-                in_=raw[:, :, c0:c1].rearrange("p t (c i) -> p c t i", i=4),
-            )
-
-        def quantise_w(w_codes, w_scales, grp):
+        def regroup_and_quantise(w):
+            regroup(nc.scalar.copy, w, 0, SCALAR_COLS[w])
+            regroup(nc.vector.tensor_copy, w, SCALAR_COLS[w], D)
             nc.vector.quantize_mx(
-                out=w_codes[:].bitcast(FP8X4), scales=w_scales[:], in_=grp[:].rearrange("p c t -> p (c t)")
+                out=w_codes[w][:].bitcast(FP8X4),
+                scales=w_scales[w][:],
+                in_=w_grouped[w][:].rearrange("p c t -> p (c t)"),
             )
 
-        def quantise(branch, b0, n):
-            assert n == 2
-            j = b0 // 2
-            nc.vector.quantize_mx(out=codes[branch][j][:].bitcast(FP8X4), scales=scales[branch][j][:], in_=grouped[branch][j][:])
-
-        def a_transpose(tag):
-            bank["aT"] = psum.tile([P, P], BF16, name="aT_ps", tag=tag)
-            nc.tensor.transpose(bank["aT"][:], a_sb[:], ident_bf[:])
-
-        def spread_bm(tag):
-            bank["bm"] = psum.tile([P, 2 * D], BF16, name="bm_ps", tag=tag)
-            for half in range(2):
-                nc.tensor.matmul(
-                    bank["bm"][:, D * half : D * half + D],
-                    lhsT=ones[:],
-                    rhs=rows[:, D * half : D * half + D],
-                    start=True,
-                    stop=True,
-                )
-
-        def front_t(j, tag):
-            oT_ps = psum.tile([P, 2, 2, P], F32, name="oT_ps%d" % j, tag=tag)
+        def transpose_o(j):
+            o_t = new_bank("front", [P, 2, 2, P], F32, "o_t%d" % j)
             words = o_sb[j][:].bitcast(F32)
             for s in range(2):
                 for u in range(2):
-                    c0 = 256 * s + P * u
-                    nc.tensor.transpose(oT_ps[:, s, u, :], words[:, c0 : c0 + P], ident_f[:])
-            bank["oT", j] = oT_ps
-
-        def exit_o(engine_copy, j):
-            engine_copy(
+                    c0 = (2 * s + u) * P
+                    nc.tensor.transpose(o_t[:, s, u, :], words[:, c0 : c0 + P], ident_f[:])
+            nc.scalar.copy(
                 out=grouped[0][j][:].bitcast(F32).rearrange("p (s i u) -> p s i u", s=2, u=2),
-                in_=bank["oT", j][:].rearrange("p s u i -> p s i u"),
+                in_=o_t[:].rearrange("p s u i -> p s i u"),
             )
 
-        def front_a(b, tag):
-            agg_ps = psum.tile([P, 4, P], F32, name="agg_ps%d" % b, tag=tag)
-            for t in range(4):
-                nc.tensor.matmul(
-                    agg_ps[:, t, :],
-                    lhsT=h_sb[b // 2][:, b % 2, P * t : P * t + P],
-                    rhs=aT_sb[:],
+        def aggregate(j):
+            agg_t = [new_bank("front", [P, PACK, P], F32, "agg_t%d" % (2 * j + s)) for s in range(2)]
+            for s in range(2):
+                for t in range(PACK):
+                    nc.tensor.matmul(
+                        agg_t[s][:, t, :], lhsT=h_sb[j][:, s, P * t : P * t + P], rhs=aT_sb[:], start=True, stop=True
+                    )
+            for s in range(2):
+                nc.scalar.copy(
+                    out=grouped[1][j][:, D * s : D * s + D].rearrange("p (i t) -> p i t", t=PACK),
+                    in_=agg_t[s][:].rearrange("p t i -> p i t"),
+                )
+
+        def quantise(branch, j):
+            nc.vector.quantize_mx(
+                out=codes[branch][j][:].bitcast(FP8X4), scales=scales[branch][j][:], in_=grouped[branch][j][:]
+            )
+
+        def product(branch, b, group):
+            j, cols = b // 2, slice(P * (b % 2), P * (b % 2) + P)
+            acc = new_bank(group, [P, D], F32, "acc%d_%d" % (branch, b))
+            nc.tensor.matmul_mx(
+                out=acc[:],
+                lhsT=codes[branch][j][:, cols].bitcast(FP8X4),
+                lhsT_scale=scales[branch][j][:, cols],
+                rhs=w_codes[branch][:].bitcast(FP8X4),
+                rhs_scale=w_scales[branch][:],
+                start=True,
+                stop=True,
+            )
+            bank[branch, b] = acc
+
+        def add_bias(b):
+            product(0, b, "proj")
+            nc.vector.tensor_tensor(out=result[b][:], in0=bank[0, b][:], in1=spread[:, 0:D], op=ADD)
+
+        def apply_gain(b):
+            product(1, b, "gcn")
+            nc.vector.tensor_tensor(out=other[b][:], in0=bank[1, b][:], in1=spread[:, D : 2 * D], op=MULT)
+
+        def join_and_store(engine, b):
+            engine.tensor_tensor(out=result[b][:], in0=result[b][:], in1=other[b][:], op=ADD)
+            store(b)
+
+        def gcn_feature_major(j):
+            halves = [new_bank("front", [P, 2, 2 * P], F32, "g_t%d_%d" % (j, half)) for half in range(2)]
+            for c in range(CHUNKS):
+                nc.tensor.matmul_mx(
+                    out=halves[c // 2][:, c % 2, :],
+                    lhsT=w_codes[1][:, P * c : P * c + P].bitcast(FP8X4),
+                    lhsT_scale=w_scales[1][:, P * c : P * c + P],
+                    rhs=codes[1][j][:].bitcast(FP8X4),
+                    rhs_scale=scales[1][j][:],
                     start=True,
                     stop=True,
                 )
-            bank["ag", b] = agg_ps
+            for c in range(CHUNKS):
+                nc.scalar.activation(
+                    out=scaled_t[j][:, c, :],
+                    in_=halves[c // 2][:, c % 2, :],
+                    func=IDENTITY,
+                    bias=per_feature[:, c : c + 1],
+                    scale=per_feature[:, CHUNKS + c : CHUNKS + c + 1],
+                )
 
-        def exit_a(engine_copy, b):
-            engine_copy(
-                out=grouped[1][b // 2][:, D * (b % 2) : D * (b % 2 + 1)].rearrange("p (i t) -> p i t", t=4),
-                in_=bank["ag", b][:].rearrange("p t i -> p i t"),
-            )
+        def projection_out(j):
+            for b in (2 * j, 2 * j + 1):
+                product(0, b, "front")
+            for b in (2 * j, 2 * j + 1):
+                nc.scalar.copy(out=other[b][:], in_=bank[0, b][:])
 
-        def mx(kind, branch, b, tag, w_codes, w_scales):
-            acc = psum.tile([P, D], F32, name="%s_ps%d" % (kind, b), tag=tag)
-            nc.tensor.matmul_mx(
-                out=acc[:],
-                lhsT=codes[branch][b // 2][:, P * (b % 2) : P * (b % 2) + P].bitcast(FP8X4),
-                lhsT_scale=scales[branch][b // 2][:, P * (b % 2) : P * (b % 2) + P],
-                rhs=w_codes[:].bitcast(FP8X4),
-                rhs_scale=w_scales[:],
-                start=True,
-                stop=True,
-            )
-            bank[kind, b] = acc
-
-        def mx_o(b, tag):
-            mx("o", 0, b, tag, wp_codes, wp_scales)
-
-        def mx_g(b, tag):
-            mx("g", 1, b, tag, gw_codes, gw_scales)
-
-        def bias(b):
-            nc.vector.tensor_tensor(out=u_sb[b][:], in0=bank["o", b][:], in1=bm_bc[:, 0:D], op=ADD)
-
-        def gain(b):
-            nc.vector.tensor_tensor(out=t_sb[b][:], in0=bank["g", b][:], in1=bm_bc[:, D : 2 * D], op=MULT)
-
-        def join(engine, b):
-            engine.tensor_tensor(out=u_sb[b][:], in0=u_sb[b][:], in1=t_sb[b][:], op=ADD)
-
-        def load_cols(half, vec):
-            nc.sync.dma_start(out=cols_in[4 * half : 4 * half + 4, :], in_=vec.rearrange("(c p) -> c p", p=P))
-
-        def cols_transpose(tag):
-            bank["col"] = psum.tile([P, P], BF16, name="col_ps", tag=tag)
-            nc.tensor.transpose(bank["col"][:], cols_in[:], ident_bf[:])
-
-        def mx_gt(j, c, tag):
-            if c % 2 == 0:
-                bank["gt", j, c // 2] = psum.tile([P, 2, 2 * P], F32, name="gt_ps%d_%d" % (j, c // 2), tag=tag)
-            nc.tensor.matmul_mx(
-                out=bank["gt", j, c // 2][:, c % 2, :],
-                lhsT=gw_codes[:, P * c : P * c + P].bitcast(FP8X4),
-                lhsT_scale=gw_scales[:, P * c : P * c + P],
-                rhs=codes[1][j][:].bitcast(FP8X4),
-                rhs_scale=scales[1][j][:],
-                start=True,
-                stop=True,
-            )
-
-        def gain_bias_t(j, c):
-            if j not in tT:
-                tT[j] = keep.tile([P, 4, 2 * P], F32, name="tT%d" % j)
-            nc.scalar.activation(
-                out=tT[j][:, c, :],
-                in_=bank["gt", j, c // 2][:, c % 2, :],
-                func=mybir.ActivationFunctionType.Identity,
-                bias=col_sb[:, c : c + 1],
-                scale=col_sb[:, 4 + c : 5 + c],
-            )
-
-        def back_t(b, tag):
-            x_ps = psum.tile([P, D], F32, name="x_ps%d" % b, tag=tag)
-            for c in range(4):
-                nc.tensor.transpose(x_ps[:, P * c : P * c + P], tT[b // 2][:, c, P * (b % 2) : P * (b % 2) + P], ident_f[:])
-            bank["x", b] = x_ps
-
-        def exit_proj(engine_copy, b):
-            ox[b] = keep.tile([P, D], F32, name="ox%d" % b)
-            engine_copy(out=ox[b][:], in_=bank["o", b][:])
-
-        def join_t(b):
-            nc.vector.tensor_tensor(out=u_sb[b][:], in0=bank["x", b][:], in1=ox[b][:], op=ADD)
-
-        def store(b):
-            nc.sync.dma_start(out=out[b], in_=u_sb[b][:])
+        def turn_back_join_store(b):
+            back = new_bank("front", [P, D], F32, "back%d" % b)
+            cols = slice(P * (b % 2), P * (b % 2) + P)
+            for c in range(CHUNKS):
+                nc.tensor.transpose(back[:, P * c : P * c + P], scaled_t[b // 2][:, c, cols], ident_f[:])
+            nc.vector.tensor_tensor(out=result[b][:], in0=back[:], in1=other[b][:], op=ADD)
+            store(b)
 
         nc.vector.memset(rows[:], 0.0)
+        nc.vector.memset(ones[:], 1.0)
+        nc.vector.memset(chunk_rows[:], 0.0)
         make_identity(nc, ident_f[:])
-        load_wp()
+        make_identity(nc, ident_bf[:])
+
+        load_weight(0)
         nc.scalar.dma_start(out=a_sb[:], in_=a_gcn)
         load_o(0)
-        load_gw()
+        load_weight(1)
         load_h(0)
         load_o(1)
         nc.scalar.dma_start(out=rows[0:1, 0:D], in_=b_proj.rearrange("(o n) -> o n", o=1))
-        make_identity(nc, ident_bf[:])
         nc.scalar.dma_start(out=rows[0:1, D : 2 * D], in_=gcn_m.rearrange("(o n) -> o n", o=1))
-        nc.scalar.activation(out=warm[:], in_=ident_f[:, 0:1], func=mybir.ActivationFunctionType.Identity)
-        a_transpose("F0")
-        regroup(nc.vector.tensor_copy, wp_grp, wp_raw, 160, D)
+        nc.scalar.activation(out=warm[:], in_=ident_f[:, 0:1], func=IDENTITY)
         load_h(1)
-        regroup(nc.scalar.copy, wp_grp, wp_raw, 0, 160)
-        load_o(2)
-        load_h(2)
-        load_o(3)
-        load_h(3)
-        front_t(0, "F1")
-        nc.scalar.copy(out=aT_sb[:], in_=bank["aT"][:])
-        nc.vector.memset(ones[:], 1.0)
-        quantise_w(wp_codes, wp_scales, wp_grp)
-        spread_bm("G0")
-        exit_o(nc.scalar.copy, 0)
-        load_o(4)
-        regroup(nc.scalar.copy, gw_grp, gw_raw, 0, 128)
-        quantise(0, 0, 2)
-        nc.vector.memset(cols_in[:], 0.0)
-        regroup(nc.vector.tensor_copy, gw_grp, gw_raw, 128, D)
-        nc.scalar.copy(out=bm_bc[:], in_=bank["bm"][:])
-        load_h(4)
-        front_a(0, "F2")
-        mx_o(0, "O0")
-        exit_a(nc.scalar.copy, 0)
-        front_a(1, "F3")
-        quantise_w(gw_codes, gw_scales, gw_grp)
-        load_o(5)
-        front_t(1, "F0")
-        exit_a(nc.scalar.copy, 1)
-        mx_o(1, "O1")
-        bias(0)
-        load_h(5)
-        front_a(2, "F1")
-        exit_o(nc.scalar.copy, 1)
-        front_a(3, "F2")
-        quantise(1, 0, 2)
-        load_cols(0, b_proj)
-        front_t(2, "F3")
-        exit_a(nc.scalar.copy, 2)
-        quantise(0, 2, 2)
-        mx_g(0, "G1")
-        load_cols(1, gcn_m)
-        bias(1)
-        exit_a(nc.scalar.copy, 3)
-        front_a(4, "F0")
-        mx_o(2, "O0")
-        exit_o(nc.scalar.copy, 2)
-        gain(0)
-        mx_g(1, "G0")
-        mx_o(3, "O1")
-        exit_a(nc.scalar.copy, 4)
-        quantise(1, 2, 2)
-        front_a(5, "F1")
-        quantise(0, 4, 2)
-        front_t(3, "F2")
-        gain(1)
-        join(nc.gpsimd, 0)
-        exit_a(nc.scalar.copy, 5)
-        front_a(7, "F3")
-        mx_g(2, "G1")
-        bias(2)
-        exit_o(nc.scalar.copy, 3)
-        front_a(6, "F0")
-        mx_g(3, "G0")
-        gain(2)
-        exit_a(nc.scalar.copy, 7)
-        join(nc.gpsimd, 1)
-        front_t(4, "F1")
-        store(0)
-        gain(3)
-        cols_transpose("F2")
-        exit_a(nc.scalar.copy, 6)
-        mx_o(4, "O0")
-        front_a(8, "F3")
-        nc.scalar.copy(out=col_sb[:], in_=bank["col"][:, 0:8])
-        exit_o(nc.scalar.copy, 4)
-        join(nc.gpsimd, 2)
-        bias(4)
-        front_a(9, "F0")
-        store(1)
-        front_t(5, "F2")
-        exit_a(nc.scalar.copy, 8)
-        bias(3)
-        front_a(10, "F1")
-        mx_o(5, "O0")
-        exit_a(nc.scalar.copy, 9)
-        quantise(1, 4, 2)
-        front_a(11, "F3")
-        store(2)
-        quantise(0, 6, 2)
-        exit_o(nc.scalar.copy, 5)
-        mx_g(4, "G1")
-        quantise(0, 8, 2)
-        mx_g(5, "G0")
-        quantise(1, 8, 2)
-        exit_a(nc.scalar.copy, 10)
-        mx_o(8, "F0")
-        quantise(1, 6, 2)
-        mx_gt(4, 2, "F2")
-        quantise(0, 10, 2)
-        exit_proj(nc.scalar.copy, 8)
-        gain(4)
-        join(nc.gpsimd, 3)
-        mx_o(9, "F1")
-        mx_o(6, "O1")
-        exit_proj(nc.scalar.copy, 9)
-        gain(5)
-        mx_gt(4, 3, None)
-        mx_g(6, "G1")
-        gain_bias_t(4, 3)
-        bias(5)
-        join(nc.gpsimd, 4)
-        mx_g(7, "G0")
-        store(3)
-        gain_bias_t(4, 2)
-        mx_o(10, "F0")
-        gain(6)
-        mx_gt(4, 0, "F1")
-        exit_a(nc.scalar.copy, 11)
-        mx_gt(4, 1, None)
-        mx_o(7, "O0")
-        gain(7)
-        join(nc.gpsimd, 5)
-        mx_o(11, "F2")
-        gain_bias_t(4, 0)
-        store(4)
-        bias(6)
-        gain_bias_t(4, 1)
-        exit_proj(nc.scalar.copy, 11)
-        quantise(1, 10, 2)
-        store(5)
-        exit_proj(nc.vector.tensor_copy, 10)
-        join(nc.gpsimd, 6)
-        mx_gt(5, 0, "F3")
-        mx_gt(5, 1, None)
-        mx_gt(5, 2, "F1")
-        bias(7)
-        mx_gt(5, 3, None)
-        gain_bias_t(5, 1)
-        back_t(8, "F2")
-        join(nc.vector, 7)
-        gain_bias_t(5, 0)
-        back_t(9, "F0")
-        store(6)
-        gain_bias_t(5, 2)
-        join_t(8)
-        store(7)
-        gain_bias_t(5, 3)
-        join_t(9)
-        store(8)
-        back_t(10, "F3")
-        back_t(11, "F2")
-        store(9)
-        join_t(10)
-        join_t(11)
-        store(10)
-        store(11)
+        for j in range(2, PAIRS):
+            load_o(j)
+            load_h(j)
+        nc.sync.dma_start(out=chunk_rows[0:CHUNKS, :], in_=b_proj.rearrange("(c p) -> c p", p=P))
+        nc.sync.dma_start(out=chunk_rows[CHUNKS : 2 * CHUNKS, :], in_=gcn_m.rearrange("(c p) -> c p", p=P))
+
+        regroup_and_quantise(0)
+        transpose_o(0)
+        a_t = new_bank("front", [P, P], BF16, "a_t")
+        nc.tensor.transpose(a_t[:], a_sb[:], ident_bf[:])
+        nc.scalar.copy(out=aT_sb[:], in_=a_t[:])
+        spread_ps = new_bank("gcn", [P, 2 * D], BF16, "spread_ps")
+        for half in range(2):
+            cols = slice(D * half, D * half + D)
+            nc.tensor.matmul(spread_ps[:, cols], lhsT=ones[:], rhs=rows[:, cols], start=True, stop=True)
+        nc.scalar.copy(out=spread[:], in_=spread_ps[:])
+        quantise(0, 0)
+        regroup_and_quantise(1)
+
+        for t in range(PAIRS):
+            aggregate(t)
+            add_bias(t)
+            if t + 1 < PAIRS:
+                transpose_o(t + 1)
+            if t >= 1:
+                apply_gain(t - 1)
+                join_and_store(nc.gpsimd, t - 1)
+            if t == PAIRS - 2:
+                chunk_cols = new_bank("front", [P, P], BF16, "chunk_cols")
+                nc.tensor.transpose(chunk_cols[:], chunk_rows[:], ident_bf[:])
+                nc.scalar.copy(out=per_feature[:], in_=chunk_cols[:, 0 : 2 * CHUNKS])
+            quantise(1, t)
+            if t + 1 < PAIRS:
+                quantise(0, t + 1)
+
+        gcn_feature_major(4)
+        add_bias(6)
+        apply_gain(5)
+        join_and_store(nc.gpsimd, 5)
+        projection_out(4)
+        add_bias(7)
+        apply_gain(6)
+        gcn_feature_major(5)
+        apply_gain(7)
+        projection_out(5)
+        for b in VECTOR_JOINS:
+            join_and_store(nc.vector, b)
+        for b in range(NODE_MAJOR, B):
+            turn_back_join_store(b)

@@ -23,6 +23,7 @@ FLOPS = 2 * 2 * B * P * D * D + 2 * B * P * P * D
 
 SCALAR_COLS = (160, 128)
 VECTOR_JOINS = (6, 7)
+BIAS_HALVES = (2, 2, 3, 3, 3, 3)
 BANKS = {"front": 4, "proj": 2, "gcn": 2}
 
 
@@ -151,17 +152,17 @@ def tile_gatblock_pa_kernel(tc, h_norm, o_attn, a_gcn, w_proj, b_proj, gcn_w, gc
             )
             bank[branch, b] = acc
 
-        def add_bias(b):
-            product(0, b, "proj")
-            nc.vector.tensor_tensor(out=result[b][:], in0=bank[0, b][:], in1=spread[:, 0:D], op=ADD)
+        def add_bias(b, c0, c1):
+            if c0 == 0:
+                product(0, b, "proj")
+            nc.vector.tensor_tensor(out=result[b][:, c0:c1], in0=bank[0, b][:, c0:c1], in1=spread[:, c0:c1], op=ADD)
 
         def apply_gain(b):
             product(1, b, "gcn")
             nc.vector.tensor_tensor(out=other[b][:], in0=bank[1, b][:], in1=spread[:, D : 2 * D], op=MULT)
 
-        def join_and_store(engine, b):
+        def join(engine, b):
             engine.tensor_tensor(out=result[b][:], in0=result[b][:], in1=other[b][:], op=ADD)
-            store(b)
 
         def gcn_feature_major(j):
             halves = [new_bank("front", [P, 2, 2 * P], F32, "g_t%d_%d" % (j, half)) for half in range(2)]
@@ -233,14 +234,25 @@ def tile_gatblock_pa_kernel(tc, h_norm, o_attn, a_gcn, w_proj, b_proj, gcn_w, gc
         quantise(0, 0)
         regroup_and_quantise(1)
 
+        halves_done = 0
         for t in range(PAIRS):
             aggregate(t)
-            add_bias(t)
+            runs = []
+            for half in range(halves_done, halves_done + BIAS_HALVES[t]):
+                if half % 2 == 1 and runs and runs[-1][0] == half // 2:
+                    runs[-1] = (half // 2, 0, D)
+                else:
+                    runs.append((half // 2, D // 2 * (half % 2), D // 2 * (half % 2 + 1)))
+            halves_done = halves_done + BIAS_HALVES[t]
+            add_bias(*runs[0])
             if t + 1 < PAIRS:
                 transpose_o(t + 1)
+            for run in runs[1:]:
+                add_bias(*run)
             if t >= 1:
                 apply_gain(t - 1)
-                join_and_store(nc.gpsimd, t - 1)
+                join(nc.gpsimd, t - 1)
+                store(t - 1)
             if t == PAIRS - 2:
                 chunk_cols = new_bank("front", [P, P], BF16, "chunk_cols")
                 nc.tensor.transpose(chunk_cols[:], chunk_rows[:], ident_bf[:])
@@ -250,16 +262,18 @@ def tile_gatblock_pa_kernel(tc, h_norm, o_attn, a_gcn, w_proj, b_proj, gcn_w, gc
                 quantise(0, t + 1)
 
         gcn_feature_major(4)
-        add_bias(6)
         apply_gain(5)
-        join_and_store(nc.gpsimd, 5)
+        join(nc.gpsimd, 5)
         projection_out(4)
-        add_bias(7)
         apply_gain(6)
         gcn_feature_major(5)
+        turn_back_join_store(8)
+        turn_back_join_store(9)
+        store(5)
         apply_gain(7)
         projection_out(5)
         for b in VECTOR_JOINS:
-            join_and_store(nc.vector, b)
-        for b in range(NODE_MAJOR, B):
-            turn_back_join_store(b)
+            join(nc.vector, b)
+            store(b)
+        turn_back_join_store(10)
+        turn_back_join_store(11)

from contextlib import ExitStack

import concourse.mybir as mybir
from concourse.masks import make_identity

FP8X4 = mybir.dt.float8_e4m3fn_x4
BF16 = mybir.dt.bfloat16
F32 = mybir.dt.float32
U32 = mybir.dt.uint32
U8 = mybir.dt.uint8
ADD = mybir.AluOpType.add
MULT = mybir.AluOpType.mult
IDENTITY = mybir.ActivationFunctionType.Identity

P = 128
D = 512
PACK = 4
B = 12
PAIRS = B // 2
CHUNKS = D // P
NODE_MAJOR = 8
FLOPS = 2 * 2 * B * P * D * D + 2 * B * P * P * D

SCALAR_COLS = (160, 128)
VECTOR_JOINS = (6, 7)
BIAS_HALVES = (2, 2, 3, 3, 3, 3)
BANKS = {"front": 4, "proj": 2, "gcn": 2}


def tile_gatblock_pa_kernel(tc, h_norm, o_attn, a_gcn, w_proj, b_proj, gcn_w, gcn_m, out):
    nc = tc.nc
    with ExitStack() as ctx:
        sbuf = ctx.enter_context(tc.tile_pool(name="sbuf", bufs=1))
        psum = ctx.enter_context(tc.psum_pool(name="psum", bufs=1))
        ctx.enter_context(tc.manual_schedule())

        ident_f = sbuf.tile([P, P], F32, name="ident_f")
        ident_bf = sbuf.tile([P, P], BF16, name="ident_bf")
        ones = sbuf.tile([P, P], BF16, name="ones")
        rows = sbuf.tile([P, 2 * D], BF16, name="rows")
        spread = sbuf.tile([P, 2 * D], BF16, name="spread")
        chunk_rows = sbuf.tile([P, P], BF16, name="chunk_rows")
        per_feature = sbuf.tile([P, 2 * CHUNKS], F32, name="per_feature")
        warm = sbuf.tile([P, 1], F32, name="warm")
        a_sb = sbuf.tile([P, P], BF16, name="a_sb")
        aT_sb = sbuf.tile([P, P], BF16, name="aT_sb")
        w_dram = (w_proj, gcn_w)
        w_raw = [sbuf.tile([P, PACK, D], BF16, name="w_raw%d" % w) for w in range(2)]
        w_grouped = [sbuf.tile([P, D, PACK], BF16, name="w_grouped%d" % w, align_bytes=64) for w in range(2)]
        w_codes = [sbuf.tile([P, D], U32, name="w_codes%d" % w, align_bytes=64) for w in range(2)]
        w_scales = [sbuf.tile([P, D], U8, name="w_scales%d" % w, align_bytes=64) for w in range(2)]
        o_sb = [sbuf.tile([P, 2 * D], BF16, name="o_sb%d" % j) for j in range(PAIRS)]
        h_sb = [sbuf.tile([P, 2, D], BF16, name="h_sb%d" % j) for j in range(PAIRS)]
        grouped = [
            [sbuf.tile([P, 2 * D], BF16, name="grouped%d_%d" % (k, j), align_bytes=64) for j in range(PAIRS)]
            for k in range(2)
        ]
        codes = [
            [sbuf.tile([P, 2 * P], U32, name="codes%d_%d" % (k, j), align_bytes=64) for j in range(PAIRS)]
            for k in range(2)
        ]
        scales = [
            [sbuf.tile([P, 2 * P], U8, name="scales%d_%d" % (k, j), align_bytes=64) for j in range(PAIRS)]
            for k in range(2)
        ]
        result = [sbuf.tile([P, D], F32, name="result%d" % b) for b in range(B)]
        other = [sbuf.tile([P, D], F32, name="other%d" % b) for b in range(B)]
        scaled_t = {j: sbuf.tile([P, CHUNKS, 2 * P], F32, name="scaled_t%d" % j) for j in range(NODE_MAJOR // 2, PAIRS)}
        bank = {}
        taken = {group: 0 for group in BANKS}

        def new_bank(group, shape, dtype, name):
            tag = "%s%d" % (group, taken[group] % BANKS[group])
            taken[group] = taken[group] + 1
            return psum.tile(shape, dtype, name=name, tag=tag)

        def load_weight(w):
            if w == 0:
                view = w_dram[w].rearrange("(u p e) c -> p u e c", u=2, p=P, e=2)
                nc.sync.dma_start(out=w_raw[w][:].rearrange("p (u e) c -> p u e c", u=2), in_=view)
            else:
                nc.sync.dma_start(out=w_raw[w][:], in_=w_dram[w].rearrange("(t p) c -> p t c", t=PACK, p=P))

        def load_o(j):
            nc.sync.dma_start(
                out=o_sb[j][:].rearrange("p (s d) -> p s d", s=2),
                in_=o_attn[2 * j : 2 * j + 2].rearrange("s n d -> n s d"),
            )

        def load_h(j):
            nc.sync.dma_start(out=h_sb[j][:], in_=h_norm[2 * j : 2 * j + 2].rearrange("s n d -> n s d"))

        def store(b):
            nc.sync.dma_start(out=out[b], in_=result[b][:])

        def regroup(copy, w, c0, c1):
            copy(
                out=w_grouped[w][:, c0:c1, :].rearrange("p (c i) t -> p c t i", i=4),
                in_=w_raw[w][:, :, c0:c1].rearrange("p t (c i) -> p c t i", i=4),
            )

        def regroup_and_quantise(w):
            regroup(nc.scalar.copy, w, 0, SCALAR_COLS[w])
            regroup(nc.vector.tensor_copy, w, SCALAR_COLS[w], D)
            nc.vector.quantize_mx(
                out=w_codes[w][:].bitcast(FP8X4),
                scales=w_scales[w][:],
                in_=w_grouped[w][:].rearrange("p c t -> p (c t)"),
            )

        def transpose_o(j):
            o_t = new_bank("front", [P, 2, 2, P], F32, "o_t%d" % j)
            words = o_sb[j][:].bitcast(F32)
            for s in range(2):
                for u in range(2):
                    c0 = (2 * s + u) * P
                    nc.tensor.transpose(o_t[:, s, u, :], words[:, c0 : c0 + P], ident_f[:])
            nc.scalar.copy(
                out=grouped[0][j][:].bitcast(F32).rearrange("p (s i u) -> p s i u", s=2, u=2),
                in_=o_t[:].rearrange("p s u i -> p s i u"),
            )

        def aggregate(j):
            agg_t = [new_bank("front", [P, PACK, P], F32, "agg_t%d" % (2 * j + s)) for s in range(2)]
            for s in range(2):
                for t in range(PACK):
                    nc.tensor.matmul(
                        agg_t[s][:, t, :], lhsT=h_sb[j][:, s, P * t : P * t + P], rhs=aT_sb[:], start=True, stop=True
                    )
            for s in range(2):
                nc.scalar.copy(
                    out=grouped[1][j][:, D * s : D * s + D].rearrange("p (i t) -> p i t", t=PACK),
                    in_=agg_t[s][:].rearrange("p t i -> p i t"),
                )

        def quantise(branch, j):
            nc.vector.quantize_mx(
                out=codes[branch][j][:].bitcast(FP8X4), scales=scales[branch][j][:], in_=grouped[branch][j][:]
            )

        def product(branch, b, group):
            j, cols = b // 2, slice(P * (b % 2), P * (b % 2) + P)
            acc = new_bank(group, [P, D], F32, "acc%d_%d" % (branch, b))
            nc.tensor.matmul_mx(
                out=acc[:],
                lhsT=codes[branch][j][:, cols].bitcast(FP8X4),
                lhsT_scale=scales[branch][j][:, cols],
                rhs=w_codes[branch][:].bitcast(FP8X4),
                rhs_scale=w_scales[branch][:],
                start=True,
                stop=True,
            )
            bank[branch, b] = acc

        def add_bias(b, c0, c1):
            if c0 == 0:
                product(0, b, "proj")
            nc.vector.tensor_tensor(out=result[b][:, c0:c1], in0=bank[0, b][:, c0:c1], in1=spread[:, c0:c1], op=ADD)

        def apply_gain(b):
            product(1, b, "gcn")
            nc.vector.tensor_tensor(out=other[b][:], in0=bank[1, b][:], in1=spread[:, D : 2 * D], op=MULT)

        def join(engine, b):
            engine.tensor_tensor(out=result[b][:], in0=result[b][:], in1=other[b][:], op=ADD)

        def gcn_feature_major(j):
            halves = [new_bank("front", [P, 2, 2 * P], F32, "g_t%d_%d" % (j, half)) for half in range(2)]
            for c in range(CHUNKS):
                nc.tensor.matmul_mx(
                    out=halves[c // 2][:, c % 2, :],
                    lhsT=w_codes[1][:, P * c : P * c + P].bitcast(FP8X4),
                    lhsT_scale=w_scales[1][:, P * c : P * c + P],
                    rhs=codes[1][j][:].bitcast(FP8X4),
                    rhs_scale=scales[1][j][:],
                    start=True,
                    stop=True,
                )
            for c in range(CHUNKS):
                nc.scalar.activation(
                    out=scaled_t[j][:, c, :],
                    in_=halves[c // 2][:, c % 2, :],
                    func=IDENTITY,
                    bias=per_feature[:, c : c + 1],
                    scale=per_feature[:, CHUNKS + c : CHUNKS + c + 1],
                )

        def projection_out(j):
            for b in (2 * j, 2 * j + 1):
                product(0, b, "front")
            for b in (2 * j, 2 * j + 1):
                nc.scalar.copy(out=other[b][:], in_=bank[0, b][:])

        def turn_back_join_store(b):
            back = new_bank("front", [P, D], F32, "back%d" % b)
            cols = slice(P * (b % 2), P * (b % 2) + P)
            for c in range(CHUNKS):
                nc.tensor.transpose(back[:, P * c : P * c + P], scaled_t[b // 2][:, c, cols], ident_f[:])
            nc.vector.tensor_tensor(out=result[b][:], in0=back[:], in1=other[b][:], op=ADD)
            store(b)

        nc.vector.memset(rows[:], 0.0)
        nc.vector.memset(ones[:], 1.0)
        nc.vector.memset(chunk_rows[:], 0.0)
        make_identity(nc, ident_f[:])
        make_identity(nc, ident_bf[:])

        load_weight(0)
        nc.scalar.dma_start(out=a_sb[:], in_=a_gcn)
        load_o(0)
        load_weight(1)
        load_h(0)
        load_o(1)
        nc.scalar.dma_start(out=rows[0:1, 0:D], in_=b_proj.rearrange("(o n) -> o n", o=1))
        nc.scalar.dma_start(out=rows[0:1, D : 2 * D], in_=gcn_m.rearrange("(o n) -> o n", o=1))
        nc.scalar.activation(out=warm[:], in_=ident_f[:, 0:1], func=IDENTITY)
        load_h(1)
        for j in range(2, PAIRS):
            load_o(j)
            load_h(j)
        nc.sync.dma_start(out=chunk_rows[0:CHUNKS, :], in_=b_proj.rearrange("(c p) -> c p", p=P))
        nc.sync.dma_start(out=chunk_rows[CHUNKS : 2 * CHUNKS, :], in_=gcn_m.rearrange("(c p) -> c p", p=P))

        regroup_and_quantise(0)
        transpose_o(0)
        a_t = new_bank("front", [P, P], BF16, "a_t")
        nc.tensor.transpose(a_t[:], a_sb[:], ident_bf[:])
        nc.scalar.copy(out=aT_sb[:], in_=a_t[:])
        spread_ps = new_bank("gcn", [P, 2 * D], BF16, "spread_ps")
        for half in range(2):
            cols = slice(D * half, D * half + D)
            nc.tensor.matmul(spread_ps[:, cols], lhsT=ones[:], rhs=rows[:, cols], start=True, stop=True)
        nc.scalar.copy(out=spread[:], in_=spread_ps[:])
        quantise(0, 0)
        regroup_and_quantise(1)

        halves_done = 0
        for t in range(PAIRS):
            aggregate(t)
            runs = []
            for half in range(halves_done, halves_done + BIAS_HALVES[t]):
                if half % 2 == 1 and runs and runs[-1][0] == half // 2:
                    runs[-1] = (half // 2, 0, D)
                else:
                    runs.append((half // 2, D // 2 * (half % 2), D // 2 * (half % 2 + 1)))
            halves_done = halves_done + BIAS_HALVES[t]
            add_bias(*runs[0])
            if t + 1 < PAIRS:
                transpose_o(t + 1)
            for run in runs[1:]:
                add_bias(*run)
            if t >= 1:
                apply_gain(t - 1)
                join(nc.gpsimd, t - 1)
                store(t - 1)
            if t == PAIRS - 2:
                chunk_cols = new_bank("front", [P, P], BF16, "chunk_cols")
                nc.tensor.transpose(chunk_cols[:], chunk_rows[:], ident_bf[:])
                nc.scalar.copy(out=per_feature[:], in_=chunk_cols[:, 0 : 2 * CHUNKS])
            quantise(1, t)
            if t + 1 < PAIRS:
                quantise(0, t + 1)

        gcn_feature_major(4)
        apply_gain(5)
        join(nc.gpsimd, 5)
        projection_out(4)
        apply_gain(6)
        gcn_feature_major(5)
        turn_back_join_store(8)
        turn_back_join_store(9)
        store(5)
        apply_gain(7)
        projection_out(5)
        for b in VECTOR_JOINS:
            join(nc.vector, b)
            store(b)
        turn_back_join_store(10)
        turn_back_join_store(11)
